import numpy as np
import ml_dtypes

BF16 = ml_dtypes.bfloat16


def bf(x):
    return np.asarray(x, np.float32).astype(BF16)


def f32(x):
    return np.asarray(x, np.float32)


def f64(x):
    return np.asarray(x).astype(np.float64)


def striped(idx):
    return np.tile(idx.reshape(-1, 16).T, (8, 1))


E, H, CX, Q, S, N = 128, 128, 256, 3, 512, 256


def sigmoid(v):
    return 1.0 / (1.0 + np.exp(-v))


def setup_inputs():
    return {
        "emb": bf(np.random.standard_normal((E, S))),
        "w_e": bf(np.random.standard_normal((E, Q * H)) / np.sqrt(2.0 * E)),
        "ctx": bf(np.random.standard_normal((CX, N))),
        "w_ctx": bf(np.random.standard_normal((CX, Q * H)) / np.sqrt(2.0 * CX)),
        "h": bf(np.random.standard_normal((H, N))),
        "w_h": bf(np.random.standard_normal((H, Q * H)) / np.sqrt(H)),
        "b_i": f32(0.1 * np.random.standard_normal((Q * H, 1))),
        "b_h": f32(0.1 * np.random.standard_normal((Q * H, 1))),
        "offs": striped(np.random.permutation(np.tile(np.arange(S), 2))[:N]),
    }


def reference(emb, w_e, ctx, w_ctx, h, w_h, b_i, b_h, offs):
    idx = offs[:16].T.reshape(-1)
    ai = f64(w_e).T @ f64(emb)[:, idx] + f64(w_ctx).T @ f64(ctx) + f64(b_i)
    ah = f64(w_h).T @ f64(h) + f64(b_h)
    i_r, i_z, i_n = np.split(ai, Q, axis=0)
    h_r, h_z, h_n = np.split(ah, Q, axis=0)
    r = sigmoid(i_r + h_r)
    z = sigmoid(i_z + h_z)
    n = np.tanh(i_n + r * h_n)
    return (1.0 - z) * n + z * f64(h)

@@ -1,0 +1,84 @@
+import concourse.mybir as mybir
+
+BF16, F32, U16 = mybir.dt.bfloat16, mybir.dt.float32, mybir.dt.uint16
+ADD, MULT = mybir.AluOpType.add, mybir.AluOpType.mult
+SIGMOID, TANH = mybir.ActivationFunctionType.Sigmoid, mybir.ActivationFunctionType.Tanh
+
+P = 128
+S = 512
+N = 256
+R, Z, C = 0, 1, 2
+
+FLOPS = 2 * (3 * P) * N * (4 * P)
+
+
+def tile_unsupervisedsedst_kernel(tc, emb, w_e, ctx, w_ctx, h, w_h, b_i, b_h, offs, out):
+    nc = tc.nc
+    with (
+        tc.tile_pool(name="held", bufs=1) as held,
+        tc.psum_pool(name="sums", bufs=1) as sums,
+    ):
+        offsets = held.tile([P, N // 16], U16, name="offsets")
+        table = held.tile([P, S], BF16, name="table")
+        we = held.tile([P, 3 * P], BF16, name="we")
+        hid = held.tile([P, N], BF16, name="hid")
+        wh = held.tile([P, 3 * P], BF16, name="wh")
+        ctx2 = held.tile([P, 2, N], BF16, name="ctx2")
+        wc2 = held.tile([P, 2, 3 * P], BF16, name="wc2")
+        bias_i = held.tile([P, 3], F32, name="bias_i")
+        bias_h = held.tile([P, 3], F32, name="bias_h")
+
+        nc.sync.dma_start(offsets[:], offs)
+        nc.sync.dma_start(table[:], emb)
+        nc.sync.dma_start(we[:], w_e)
+        nc.sync.dma_start(ctx2[:], ctx.rearrange("(b p) n -> p b n", p=P))
+        nc.scalar.dma_start(hid[:], h)
+        nc.scalar.dma_start(wh[:], w_h)
+        nc.scalar.dma_start(wc2[:], w_ctx.rearrange("(b p) m -> p b m", p=P))
+        with nc.allow_non_contiguous_dma(reason="384 biases, one to a partition and gate"):
+            nc.sync.dma_start(bias_i[:], b_i.rearrange("(g m) o -> m (g o)", m=P))
+            nc.scalar.dma_start(bias_h[:], b_h.rearrange("(g m) o -> m (g o)", m=P))
+
+        bias_sum = held.tile([P, 3], F32, name="bias_sum")
+        nc.vector.tensor_tensor(bias_sum[:], bias_i[:], bias_h[:], ADD)
+
+        sum_r = sums.tile([P, N], F32, name="sum_r")
+        sum_z = sums.tile([P, N], F32, name="sum_z")
+        sum_ic = sums.tile([P, N], F32, name="sum_ic")
+        sum_hc = sums.tile([P, N], F32, name="sum_hc")
+        input_sums = ((R, sum_r), (C, sum_ic), (Z, sum_z))
+
+        for g, bank in input_sums:
+            nc.tensor.matmul(
+                bank[:], we[:, g * P : (g + 1) * P], table[:].indirect(offsets[:]), start=True, stop=False
+            )
+        nc.tensor.matmul(sum_r[:], wh[:, R * P : (R + 1) * P], hid[:], start=False, stop=False)
+        nc.tensor.matmul(sum_hc[:], wh[:, C * P : (C + 1) * P], hid[:], start=True, stop=True)
+        nc.tensor.matmul(sum_z[:], wh[:, Z * P : (Z + 1) * P], hid[:], start=False, stop=False)
+        for g, bank in input_sums:
+            for b in range(2):
+                nc.tensor.matmul(
+                    bank[:], wc2[:, b, g * P : (g + 1) * P], ctx2[:, b, :], start=False, stop=(b == 1)
+                )
+
+        r = held.tile([P, N], F32, name="r")
+        nc.scalar.activation(r[:], sum_r[:], SIGMOID, bias=bias_sum[:, R : R + 1])
+
+        r_hc = held.tile([P, N], F32, name="r_hc")
+        nc.vector.scalar_tensor_tensor(r_hc[:], sum_hc[:], bias_h[:, C : C + 1], r[:], ADD, MULT)
+        pre_n = held.tile([P, N], F32, name="pre_n")
+        nc.vector.tensor_tensor(pre_n[:], r_hc[:], sum_ic[:], ADD)
+        n = held.tile([P, N], F32, name="n")
+        nc.scalar.activation(n[:], pre_n[:], TANH, bias=bias_i[:, C : C + 1])
+
+        z = held.tile([P, N], F32, name="z")
+        nc.scalar.activation(z[:], sum_z[:], SIGMOID, bias=bias_sum[:, Z : Z + 1])
+        one_minus_z = held.tile([P, N], F32, name="one_minus_z")
+        nc.vector.tensor_scalar(one_minus_z[:], z[:], -1.0, 1.0, MULT, ADD)
+        z_h = held.tile([P, N], F32, name="z_h")
+        nc.vector.tensor_tensor(z_h[:], z[:], hid[:], MULT)
+
+        new_h = held.tile([P, N], F32, name="new_h")
+        nc.vector.tensor_tensor(new_h[:], one_minus_z[:], n[:], MULT)
+        nc.vector.tensor_tensor(new_h[:], new_h[:], z_h[:], ADD)
+        nc.sync.dma_start(out, new_h[:])

@@ -39,6 +39,10 @@ def tile_unsupervisedsedst_kernel(tc, emb, w_e, ctx, w_ctx, h, w_h, b_i, b_h, of
             nc.sync.dma_start(bias_i[:], b_i.rearrange("(g m) o -> m (g o)", m=P))
             nc.scalar.dma_start(bias_h[:], b_h.rearrange("(g m) o -> m (g o)", m=P))
 
+        early = held.tile([P, 1], F32, name="early")
+        nc.vector.memset(early[:], 0.0)
+        nc.scalar.activation(early[:], early[:], SIGMOID)
+
         bias_sum = held.tile([P, 3], F32, name="bias_sum")
         nc.vector.tensor_tensor(bias_sum[:], bias_i[:], bias_h[:], ADD)
 

@@ -9,6 +9,8 @@ S = 512
 N = 256
 R, Z, C = 0, 1, 2
 
+WARM = 8
+
 FLOPS = 2 * (3 * P) * N * (4 * P)
 
 
@@ -18,6 +20,12 @@ def tile_unsupervisedsedst_kernel(tc, emb, w_e, ctx, w_ctx, h, w_h, b_i, b_h, of
         tc.tile_pool(name="held", bufs=1) as held,
         tc.psum_pool(name="sums", bufs=1) as sums,
     ):
+        zeros = held.tile([P, N], BF16, name="zeros")
+        nc.vector.memset(zeros[:], 0.0)
+        unread = sums.tile([P, N], F32, name="unread")
+        for k in range(WARM):
+            nc.tensor.matmul(unread[:], zeros[:, 0:P], zeros[:], start=True, stop=True)
+
         offsets = held.tile([P, N // 16], U16, name="offsets")
         table = held.tile([P, S], BF16, name="table")
         we = held.tile([P, 3 * P], BF16, name="we")
@@ -67,6 +75,8 @@ def tile_unsupervisedsedst_kernel(tc, emb, w_e, ctx, w_ctx, h, w_h, b_i, b_h, of
 
         r = held.tile([P, N], F32, name="r")
         nc.scalar.activation(r[:], sum_r[:], SIGMOID, bias=bias_sum[:, R : R + 1])
+        z = held.tile([P, N], F32, name="z")
+        nc.scalar.activation(z[:], sum_z[:], SIGMOID, bias=bias_sum[:, Z : Z + 1])
 
         r_hc = held.tile([P, N], F32, name="r_hc")
         nc.vector.scalar_tensor_tensor(r_hc[:], sum_hc[:], bias_h[:, C : C + 1], r[:], ADD, MULT)
@@ -75,8 +85,6 @@ def tile_unsupervisedsedst_kernel(tc, emb, w_e, ctx, w_ctx, h, w_h, b_i, b_h, of
         n = held.tile([P, N], F32, name="n")
         nc.scalar.activation(n[:], pre_n[:], TANH, bias=bias_i[:, C : C + 1])
 
-        z = held.tile([P, N], F32, name="z")
-        nc.scalar.activation(z[:], sum_z[:], SIGMOID, bias=bias_sum[:, Z : Z + 1])
         one_minus_z = held.tile([P, N], F32, name="one_minus_z")
         nc.vector.tensor_scalar(one_minus_z[:], z[:], -1.0, 1.0, MULT, ADD)
         z_h = held.tile([P, N], F32, name="z_h")

@@ -1,7 +1,7 @@
 import concourse.mybir as mybir
 
 BF16, F32, U16 = mybir.dt.bfloat16, mybir.dt.float32, mybir.dt.uint16
-ADD, MULT = mybir.AluOpType.add, mybir.AluOpType.mult
+ADD, SUBTRACT, MULT = mybir.AluOpType.add, mybir.AluOpType.subtract, mybir.AluOpType.mult
 SIGMOID, TANH = mybir.ActivationFunctionType.Sigmoid, mybir.ActivationFunctionType.Tanh
 
 P = 128
@@ -73,24 +73,33 @@ def tile_unsupervisedsedst_kernel(tc, emb, w_e, ctx, w_ctx, h, w_h, b_i, b_h, of
                     bank[:], wc2[:, b, g * P : (g + 1) * P], ctx2[:, b, :], start=False, stop=(b == 1)
                 )
 
+        halves = (slice(0, N // 2), slice(N // 2, N))
+
         r = held.tile([P, N], F32, name="r")
-        nc.scalar.activation(r[:], sum_r[:], SIGMOID, bias=bias_sum[:, R : R + 1])
+        for cols in halves:
+            nc.scalar.activation(r[:, cols], sum_r[:, cols], SIGMOID, bias=bias_sum[:, R : R + 1])
         z = held.tile([P, N], F32, name="z")
         nc.scalar.activation(z[:], sum_z[:], SIGMOID, bias=bias_sum[:, Z : Z + 1])
 
         r_hc = held.tile([P, N], F32, name="r_hc")
-        nc.vector.scalar_tensor_tensor(r_hc[:], sum_hc[:], bias_h[:, C : C + 1], r[:], ADD, MULT)
+        for cols in halves:
+            nc.vector.scalar_tensor_tensor(
+                r_hc[:, cols], sum_hc[:, cols], bias_h[:, C : C + 1], r[:, cols], ADD, MULT
+            )
         pre_n = held.tile([P, N], F32, name="pre_n")
-        nc.vector.tensor_tensor(pre_n[:], r_hc[:], sum_ic[:], ADD)
+        for cols in halves:
+            nc.vector.tensor_tensor(pre_n[:, cols], r_hc[:, cols], sum_ic[:, cols], ADD)
         n = held.tile([P, N], F32, name="n")
-        nc.scalar.activation(n[:], pre_n[:], TANH, bias=bias_i[:, C : C + 1])
+        for cols in halves:
+            nc.scalar.activation(n[:, cols], pre_n[:, cols], TANH, bias=bias_i[:, C : C + 1])
 
-        one_minus_z = held.tile([P, N], F32, name="one_minus_z")
-        nc.vector.tensor_scalar(one_minus_z[:], z[:], -1.0, 1.0, MULT, ADD)
         z_h = held.tile([P, N], F32, name="z_h")
         nc.vector.tensor_tensor(z_h[:], z[:], hid[:], MULT)
-
+        z1_n = held.tile([P, N], F32, name="z1_n")
+        for cols in halves:
+            nc.vector.scalar_tensor_tensor(z1_n[:, cols], z[:, cols], 1.0, n[:, cols], SUBTRACT, MULT)
         new_h = held.tile([P, N], F32, name="new_h")
-        nc.vector.tensor_tensor(new_h[:], one_minus_z[:], n[:], MULT)
-        nc.vector.tensor_tensor(new_h[:], new_h[:], z_h[:], ADD)
-        nc.sync.dma_start(out, new_h[:])
+        for cols in halves:
+            nc.vector.tensor_tensor(new_h[:, cols], z_h[:, cols], z1_n[:, cols], SUBTRACT)
+        for cols, queue in zip(halves, (nc.sync, nc.scalar)):
+            queue.dma_start(out[:, cols], new_h[:, cols])

@@ -1,4 +1,5 @@
 import concourse.mybir as mybir
+from concourse.masks import make_identity
 
 BF16, F32, U16 = mybir.dt.bfloat16, mybir.dt.float32, mybir.dt.uint16
 ADD, SUBTRACT, MULT = mybir.AluOpType.add, mybir.AluOpType.subtract, mybir.AluOpType.mult
@@ -33,9 +34,10 @@ def tile_unsupervisedsedst_kernel(tc, emb, w_e, ctx, w_ctx, h, w_h, b_i, b_h, of
         wh = held.tile([P, 3 * P], BF16, name="wh")
         ctx2 = held.tile([P, 2, N], BF16, name="ctx2")
         wc2 = held.tile([P, 2, 3 * P], BF16, name="wc2")
-        bias_i = held.tile([P, 3], F32, name="bias_i")
-        bias_h = held.tile([P, 3], F32, name="bias_h")
+        bias_rows = held.tile([2 * 3, P], F32, name="bias_rows")
 
+        nc.sync.dma_start(bias_rows[0:3, :], b_i.rearrange("(g m) o -> g (m o)", m=P))
+        nc.scalar.dma_start(bias_rows[3:6, :], b_h.rearrange("(g m) o -> g (m o)", m=P))
         nc.sync.dma_start(offsets[:], offs)
         nc.sync.dma_start(table[:], emb)
         nc.sync.dma_start(we[:], w_e)
@@ -43,16 +45,20 @@ def tile_unsupervisedsedst_kernel(tc, emb, w_e, ctx, w_ctx, h, w_h, b_i, b_h, of
         nc.scalar.dma_start(hid[:], h)
         nc.scalar.dma_start(wh[:], w_h)
         nc.scalar.dma_start(wc2[:], w_ctx.rearrange("(b p) m -> p b m", p=P))
-        with nc.allow_non_contiguous_dma(reason="384 biases, one to a partition and gate"):
-            nc.sync.dma_start(bias_i[:], b_i.rearrange("(g m) o -> m (g o)", m=P))
-            nc.scalar.dma_start(bias_h[:], b_h.rearrange("(g m) o -> m (g o)", m=P))
 
         early = held.tile([P, 1], F32, name="early")
         nc.vector.memset(early[:], 0.0)
         nc.scalar.activation(early[:], early[:], SIGMOID)
 
+        identity = held.tile([2 * 3, 2 * 3], F32, name="identity")
+        make_identity(nc, identity[:])
+        bias_turned = sums.tile([P, 2 * 3], F32, name="bias_turned")
+        nc.tensor.matmul(bias_turned[:], bias_rows[:], identity[:], start=True, stop=True)
+        bias = held.tile([P, 2 * 3], F32, name="bias")
+        nc.vector.tensor_copy(bias[:], bias_turned[:])
+        bias_i, bias_h = bias[:, 0:3], bias[:, 3:6]
         bias_sum = held.tile([P, 3], F32, name="bias_sum")
-        nc.vector.tensor_tensor(bias_sum[:], bias_i[:], bias_h[:], ADD)
+        nc.vector.tensor_tensor(bias_sum[:], bias_i, bias_h, ADD)
 
         sum_r = sums.tile([P, N], F32, name="sum_r")
         sum_z = sums.tile([P, N], F32, name="sum_z")

@@ -40,10 +40,10 @@ def tile_unsupervisedsedst_kernel(tc, emb, w_e, ctx, w_ctx, h, w_h, b_i, b_h, of
         nc.scalar.dma_start(bias_rows[3:6, :], b_h.rearrange("(g m) o -> g (m o)", m=P))
         nc.sync.dma_start(offsets[:], offs)
         nc.sync.dma_start(table[:], emb)
-        nc.sync.dma_start(we[:], w_e)
-        nc.sync.dma_start(ctx2[:], ctx.rearrange("(b p) n -> p b n", p=P))
-        nc.scalar.dma_start(hid[:], h)
+        nc.scalar.dma_start(we[:], w_e)
+        nc.sync.dma_start(hid[:], h)
         nc.scalar.dma_start(wh[:], w_h)
+        nc.sync.dma_start(ctx2[:], ctx.rearrange("(b p) n -> p b n", p=P))
         nc.scalar.dma_start(wc2[:], w_ctx.rearrange("(b p) m -> p b m", p=P))
 
         early = held.tile([P, 1], F32, name="early")

@@ -1,5 +1,4 @@
 import concourse.mybir as mybir
-from concourse.masks import make_identity
 
 BF16, F32, U16 = mybir.dt.bfloat16, mybir.dt.float32, mybir.dt.uint16
 ADD, SUBTRACT, MULT = mybir.AluOpType.add, mybir.AluOpType.subtract, mybir.AluOpType.mult
@@ -34,31 +33,26 @@ def tile_unsupervisedsedst_kernel(tc, emb, w_e, ctx, w_ctx, h, w_h, b_i, b_h, of
         wh = held.tile([P, 3 * P], BF16, name="wh")
         ctx2 = held.tile([P, 2, N], BF16, name="ctx2")
         wc2 = held.tile([P, 2, 3 * P], BF16, name="wc2")
-        bias_rows = held.tile([2 * 3, P], F32, name="bias_rows")
+        bias_i = held.tile([P, 3], F32, name="bias_i")
+        bias_h = held.tile([P, 3], F32, name="bias_h")
 
-        nc.sync.dma_start(bias_rows[0:3, :], b_i.rearrange("(g m) o -> g (m o)", m=P))
-        nc.scalar.dma_start(bias_rows[3:6, :], b_h.rearrange("(g m) o -> g (m o)", m=P))
         nc.sync.dma_start(offsets[:], offs)
         nc.sync.dma_start(table[:], emb)
         nc.scalar.dma_start(we[:], w_e)
-        nc.sync.dma_start(hid[:], h)
+        nc.gpsimd.dma_start(hid[:], h)
         nc.scalar.dma_start(wh[:], w_h)
         nc.sync.dma_start(ctx2[:], ctx.rearrange("(b p) n -> p b n", p=P))
         nc.scalar.dma_start(wc2[:], w_ctx.rearrange("(b p) m -> p b m", p=P))
+        with nc.allow_non_contiguous_dma(reason="384 biases, one to a partition and gate"):
+            nc.sync.dma_start(bias_i[:], b_i.rearrange("(g m) o -> m (g o)", m=P))
+            nc.scalar.dma_start(bias_h[:], b_h.rearrange("(g m) o -> m (g o)", m=P))
 
         early = held.tile([P, 1], F32, name="early")
         nc.vector.memset(early[:], 0.0)
         nc.scalar.activation(early[:], early[:], SIGMOID)
 
-        identity = held.tile([2 * 3, 2 * 3], F32, name="identity")
-        make_identity(nc, identity[:])
-        bias_turned = sums.tile([P, 2 * 3], F32, name="bias_turned")
-        nc.tensor.matmul(bias_turned[:], bias_rows[:], identity[:], start=True, stop=True)
-        bias = held.tile([P, 2 * 3], F32, name="bias")
-        nc.vector.tensor_copy(bias[:], bias_turned[:])
-        bias_i, bias_h = bias[:, 0:3], bias[:, 3:6]
         bias_sum = held.tile([P, 3], F32, name="bias_sum")
-        nc.vector.tensor_tensor(bias_sum[:], bias_i, bias_h, ADD)
+        nc.vector.tensor_tensor(bias_sum[:], bias_i[:], bias_h[:], ADD)
 
         sum_r = sums.tile([P, N], F32, name="sum_r")
         sum_z = sums.tile([P, N], F32, name="sum_z")

@@ -7,11 +7,13 @@ SIGMOID, TANH = mybir.ActivationFunctionType.Sigmoid, mybir.ActivationFunctionTy
 P = 128
 S = 512
 N = 256
+GATES = 3
 R, Z, C = 0, 1, 2
+CTX_BLOCKS = 2
 
 WARM = 8
 
-FLOPS = 2 * (3 * P) * N * (4 * P)
+FLOPS = 2 * (GATES * P) * N * ((1 + CTX_BLOCKS + 1) * P)
 
 
 def tile_unsupervisedsedst_kernel(tc, emb, w_e, ctx, w_ctx, h, w_h, b_i, b_h, offs, out):
@@ -28,20 +30,20 @@ def tile_unsupervisedsedst_kernel(tc, emb, w_e, ctx, w_ctx, h, w_h, b_i, b_h, of
 
         offsets = held.tile([P, N // 16], U16, name="offsets")
         table = held.tile([P, S], BF16, name="table")
-        we = held.tile([P, 3 * P], BF16, name="we")
+        we = held.tile([P, GATES * P], BF16, name="we")
         hid = held.tile([P, N], BF16, name="hid")
-        wh = held.tile([P, 3 * P], BF16, name="wh")
-        ctx2 = held.tile([P, 2, N], BF16, name="ctx2")
-        wc2 = held.tile([P, 2, 3 * P], BF16, name="wc2")
-        bias_i = held.tile([P, 3], F32, name="bias_i")
-        bias_h = held.tile([P, 3], F32, name="bias_h")
+        wh = held.tile([P, GATES * P], BF16, name="wh")
+        ctx2 = held.tile([P, CTX_BLOCKS, N], BF16, name="ctx2")
+        wc2 = held.tile([P, CTX_BLOCKS, GATES * P], BF16, name="wc2")
+        bias_i = held.tile([P, GATES], F32, name="bias_i")
+        bias_h = held.tile([P, GATES], F32, name="bias_h")
 
         nc.sync.dma_start(offsets[:], offs)
         nc.sync.dma_start(table[:], emb)
         nc.scalar.dma_start(we[:], w_e)
-        nc.gpsimd.dma_start(hid[:], h)
+        nc.sync.dma_start(hid[:], h)
         nc.scalar.dma_start(wh[:], w_h)
-        nc.sync.dma_start(ctx2[:], ctx.rearrange("(b p) n -> p b n", p=P))
+        nc.sync.dma_start(ctx2[:], ctx.rearrange("(b p) j -> p b j", p=P))
         nc.scalar.dma_start(wc2[:], w_ctx.rearrange("(b p) m -> p b m", p=P))
         with nc.allow_non_contiguous_dma(reason="384 biases, one to a partition and gate"):
             nc.sync.dma_start(bias_i[:], b_i.rearrange("(g m) o -> m (g o)", m=P))
@@ -51,7 +53,7 @@ def tile_unsupervisedsedst_kernel(tc, emb, w_e, ctx, w_ctx, h, w_h, b_i, b_h, of
         nc.vector.memset(early[:], 0.0)
         nc.scalar.activation(early[:], early[:], SIGMOID)
 
-        bias_sum = held.tile([P, 3], F32, name="bias_sum")
+        bias_sum = held.tile([P, GATES], F32, name="bias_sum")
         nc.vector.tensor_tensor(bias_sum[:], bias_i[:], bias_h[:], ADD)
 
         sum_r = sums.tile([P, N], F32, name="sum_r")
@@ -68,9 +70,13 @@ def tile_unsupervisedsedst_kernel(tc, emb, w_e, ctx, w_ctx, h, w_h, b_i, b_h, of
         nc.tensor.matmul(sum_hc[:], wh[:, C * P : (C + 1) * P], hid[:], start=True, stop=True)
         nc.tensor.matmul(sum_z[:], wh[:, Z * P : (Z + 1) * P], hid[:], start=False, stop=False)
         for g, bank in input_sums:
-            for b in range(2):
+            for b in range(CTX_BLOCKS):
                 nc.tensor.matmul(
-                    bank[:], wc2[:, b, g * P : (g + 1) * P], ctx2[:, b, :], start=False, stop=(b == 1)
+                    bank[:],
+                    wc2[:, b, g * P : (g + 1) * P],
+                    ctx2[:, b, :],
+                    start=False,
+                    stop=(b == CTX_BLOCKS - 1),
                 )
 
         halves = (slice(0, N // 2), slice(N // 2, N))

@@ -38,16 +38,20 @@ def tile_unsupervisedsedst_kernel(tc, emb, w_e, ctx, w_ctx, h, w_h, b_i, b_h, of
         bias_i = held.tile([P, GATES], F32, name="bias_i")
         bias_h = held.tile([P, GATES], F32, name="bias_h")
 
+        with nc.allow_non_contiguous_dma(reason="384 biases, one to a partition and gate"):
+            nc.sync.dma_start(bias_i[:], b_i.rearrange("(g m) o -> m (g o)", m=P))
+            nc.sync.dma_start(bias_h[:], b_h.rearrange("(g m) o -> m (g o)", m=P))
         nc.sync.dma_start(offsets[:], offs)
         nc.sync.dma_start(table[:], emb)
         nc.scalar.dma_start(we[:], w_e)
-        nc.sync.dma_start(hid[:], h)
-        nc.scalar.dma_start(wh[:], w_h)
+        w_ctx2 = w_ctx.rearrange("(b p) m -> p b m", p=P)
+        reset, others = slice(R * P, (R + 1) * P), slice((R + 1) * P, GATES * P)
+        nc.scalar.dma_start(hid[:], h)
+        nc.scalar.dma_start(wh[:, reset], w_h[:, reset])
         nc.sync.dma_start(ctx2[:], ctx.rearrange("(b p) j -> p b j", p=P))
-        nc.scalar.dma_start(wc2[:], w_ctx.rearrange("(b p) m -> p b m", p=P))
-        with nc.allow_non_contiguous_dma(reason="384 biases, one to a partition and gate"):
-            nc.sync.dma_start(bias_i[:], b_i.rearrange("(g m) o -> m (g o)", m=P))
-            nc.scalar.dma_start(bias_h[:], b_h.rearrange("(g m) o -> m (g o)", m=P))
+        nc.scalar.dma_start(wc2[:, :, reset], w_ctx2[:, :, reset])
+        nc.sync.dma_start(wh[:, others], w_h[:, others])
+        nc.sync.dma_start(wc2[:, :, others], w_ctx2[:, :, others])
 
         early = held.tile([P, 1], F32, name="early")
         nc.vector.memset(early[:], 0.0)
@@ -66,10 +70,11 @@ def tile_unsupervisedsedst_kernel(tc, emb, w_e, ctx, w_ctx, h, w_h, b_i, b_h, of
             nc.tensor.matmul(
                 bank[:], we[:, g * P : (g + 1) * P], table[:].indirect(offsets[:]), start=True, stop=False
             )
-        nc.tensor.matmul(sum_r[:], wh[:, R * P : (R + 1) * P], hid[:], start=False, stop=False)
-        nc.tensor.matmul(sum_hc[:], wh[:, C * P : (C + 1) * P], hid[:], start=True, stop=True)
-        nc.tensor.matmul(sum_z[:], wh[:, Z * P : (Z + 1) * P], hid[:], start=False, stop=False)
         for g, bank in input_sums:
+            if g == C:
+                nc.tensor.matmul(sum_hc[:], wh[:, g * P : (g + 1) * P], hid[:], start=True, stop=True)
+            else:
+                nc.tensor.matmul(bank[:], wh[:, g * P : (g + 1) * P], hid[:], start=False, stop=False)
             for b in range(CTX_BLOCKS):
                 nc.tensor.matmul(
                     bank[:],

@@ -10,6 +10,7 @@ N = 256
 GATES = 3
 R, Z, C = 0, 1, 2
 CTX_BLOCKS = 2
+PIECES = 4
 
 WARM = 8
 
@@ -85,32 +86,33 @@ def tile_unsupervisedsedst_kernel(tc, emb, w_e, ctx, w_ctx, h, w_h, b_i, b_h, of
                 )
 
         halves = (slice(0, N // 2), slice(N // 2, N))
+        pieces = [slice(q * N // PIECES, (q + 1) * N // PIECES) for q in range(PIECES)]
 
         r = held.tile([P, N], F32, name="r")
-        for cols in halves:
+        for cols in pieces:
             nc.scalar.activation(r[:, cols], sum_r[:, cols], SIGMOID, bias=bias_sum[:, R : R + 1])
         z = held.tile([P, N], F32, name="z")
         nc.scalar.activation(z[:], sum_z[:], SIGMOID, bias=bias_sum[:, Z : Z + 1])
 
         r_hc = held.tile([P, N], F32, name="r_hc")
-        for cols in halves:
+        for cols in pieces:
             nc.vector.scalar_tensor_tensor(
                 r_hc[:, cols], sum_hc[:, cols], bias_h[:, C : C + 1], r[:, cols], ADD, MULT
             )
         pre_n = held.tile([P, N], F32, name="pre_n")
-        for cols in halves:
+        for cols in pieces:
             nc.vector.tensor_tensor(pre_n[:, cols], r_hc[:, cols], sum_ic[:, cols], ADD)
         n = held.tile([P, N], F32, name="n")
-        for cols in halves:
+        for cols in pieces:
             nc.scalar.activation(n[:, cols], pre_n[:, cols], TANH, bias=bias_i[:, C : C + 1])
 
         z_h = held.tile([P, N], F32, name="z_h")
         nc.vector.tensor_tensor(z_h[:], z[:], hid[:], MULT)
         z1_n = held.tile([P, N], F32, name="z1_n")
-        for cols in halves:
+        for cols in pieces:
             nc.vector.scalar_tensor_tensor(z1_n[:, cols], z[:, cols], 1.0, n[:, cols], SUBTRACT, MULT)
         new_h = held.tile([P, N], F32, name="new_h")
-        for cols in halves:
+        for cols in pieces:
             nc.vector.tensor_tensor(new_h[:, cols], z_h[:, cols], z1_n[:, cols], SUBTRACT)
         for cols, queue in zip(halves, (nc.sync, nc.scalar)):
             queue.dma_start(out[:, cols], new_h[:, cols])

@@ -36,12 +36,16 @@ def tile_unsupervisedsedst_kernel(tc, emb, w_e, ctx, w_ctx, h, w_h, b_i, b_h, of
         wh = held.tile([P, GATES * P], BF16, name="wh")
         ctx2 = held.tile([P, CTX_BLOCKS, N], BF16, name="ctx2")
         wc2 = held.tile([P, CTX_BLOCKS, GATES * P], BF16, name="wc2")
-        bias_i = held.tile([P, GATES], F32, name="bias_i")
-        bias_h = held.tile([P, GATES], F32, name="bias_h")
+        bias_i_reset = held.tile([P, 1], F32, name="bias_i_reset")
+        bias_h_reset = held.tile([P, 1], F32, name="bias_h_reset")
+        bias_i_others = held.tile([P, GATES - 1], F32, name="bias_i_others")
+        bias_h_others = held.tile([P, GATES - 1], F32, name="bias_h_others")
+        b_i_cols = b_i.rearrange("(g m) o -> m (g o)", m=P)
+        b_h_cols = b_h.rearrange("(g m) o -> m (g o)", m=P)
 
-        with nc.allow_non_contiguous_dma(reason="384 biases, one to a partition and gate"):
-            nc.sync.dma_start(bias_i[:], b_i.rearrange("(g m) o -> m (g o)", m=P))
-            nc.sync.dma_start(bias_h[:], b_h.rearrange("(g m) o -> m (g o)", m=P))
+        with nc.allow_non_contiguous_dma(reason="128 biases, one to a partition"):
+            nc.sync.dma_start(bias_i_reset[:], b_i_cols[:, R : R + 1])
+            nc.sync.dma_start(bias_h_reset[:], b_h_cols[:, R : R + 1])
         nc.sync.dma_start(offsets[:], offs)
         nc.sync.dma_start(table[:], emb)
         nc.scalar.dma_start(we[:], w_e)
@@ -51,6 +55,9 @@ def tile_unsupervisedsedst_kernel(tc, emb, w_e, ctx, w_ctx, h, w_h, b_i, b_h, of
         nc.scalar.dma_start(wh[:, reset], w_h[:, reset])
         nc.sync.dma_start(ctx2[:], ctx.rearrange("(b p) j -> p b j", p=P))
         nc.scalar.dma_start(wc2[:, :, reset], w_ctx2[:, :, reset])
+        with nc.allow_non_contiguous_dma(reason="256 biases, one to a partition and gate"):
+            nc.sync.dma_start(bias_h_others[:], b_h_cols[:, R + 1 : GATES])
+            nc.sync.dma_start(bias_i_others[:], b_i_cols[:, R + 1 : GATES])
         nc.sync.dma_start(wh[:, others], w_h[:, others])
         nc.sync.dma_start(wc2[:, :, others], w_ctx2[:, :, others])
 
@@ -58,8 +65,10 @@ def tile_unsupervisedsedst_kernel(tc, emb, w_e, ctx, w_ctx, h, w_h, b_i, b_h, of
         nc.vector.memset(early[:], 0.0)
         nc.scalar.activation(early[:], early[:], SIGMOID)
 
-        bias_sum = held.tile([P, GATES], F32, name="bias_sum")
-        nc.vector.tensor_tensor(bias_sum[:], bias_i[:], bias_h[:], ADD)
+        bias_sum_reset = held.tile([P, 1], F32, name="bias_sum_reset")
+        nc.vector.tensor_tensor(bias_sum_reset[:], bias_i_reset[:], bias_h_reset[:], ADD)
+        bias_sum_others = held.tile([P, GATES - 1], F32, name="bias_sum_others")
+        nc.vector.tensor_tensor(bias_sum_others[:], bias_i_others[:], bias_h_others[:], ADD)
 
         sum_r = sums.tile([P, N], F32, name="sum_r")
         sum_z = sums.tile([P, N], F32, name="sum_z")
@@ -90,24 +99,26 @@ def tile_unsupervisedsedst_kernel(tc, emb, w_e, ctx, w_ctx, h, w_h, b_i, b_h, of
 
         r = held.tile([P, N], F32, name="r")
         for cols in pieces:
-            nc.scalar.activation(r[:, cols], sum_r[:, cols], SIGMOID, bias=bias_sum[:, R : R + 1])
+            nc.scalar.activation(r[:, cols], sum_r[:, cols], SIGMOID, bias=bias_sum_reset[:])
         z = held.tile([P, N], F32, name="z")
-        nc.scalar.activation(z[:], sum_z[:], SIGMOID, bias=bias_sum[:, Z : Z + 1])
+        for cols in pieces:
+            nc.scalar.activation(z[:, cols], sum_z[:, cols], SIGMOID, bias=bias_sum_others[:, Z - 1 : Z])
 
         r_hc = held.tile([P, N], F32, name="r_hc")
         for cols in pieces:
             nc.vector.scalar_tensor_tensor(
-                r_hc[:, cols], sum_hc[:, cols], bias_h[:, C : C + 1], r[:, cols], ADD, MULT
+                r_hc[:, cols], sum_hc[:, cols], bias_h_others[:, C - 1 : C], r[:, cols], ADD, MULT
             )
         pre_n = held.tile([P, N], F32, name="pre_n")
         for cols in pieces:
             nc.vector.tensor_tensor(pre_n[:, cols], r_hc[:, cols], sum_ic[:, cols], ADD)
         n = held.tile([P, N], F32, name="n")
         for cols in pieces:
-            nc.scalar.activation(n[:, cols], pre_n[:, cols], TANH, bias=bias_i[:, C : C + 1])
+            nc.scalar.activation(n[:, cols], pre_n[:, cols], TANH, bias=bias_i_others[:, C - 1 : C])
 
         z_h = held.tile([P, N], F32, name="z_h")
-        nc.vector.tensor_tensor(z_h[:], z[:], hid[:], MULT)
+        for cols in pieces:
+            nc.vector.tensor_tensor(z_h[:, cols], z[:, cols], hid[:, cols], MULT)
         z1_n = held.tile([P, N], F32, name="z1_n")
         for cols in pieces:
             nc.vector.scalar_tensor_tensor(z1_n[:, cols], z[:, cols], 1.0, n[:, cols], SUBTRACT, MULT)

@@ -9,6 +9,8 @@ S = 512
 N = 256
 GATES = 3
 R, Z, C = 0, 1, 2
+BLOCK = 32
+I, H = 0, 1
 CTX_BLOCKS = 2
 PIECES = 4
 
@@ -36,16 +38,10 @@ def tile_unsupervisedsedst_kernel(tc, emb, w_e, ctx, w_ctx, h, w_h, b_i, b_h, of
         wh = held.tile([P, GATES * P], BF16, name="wh")
         ctx2 = held.tile([P, CTX_BLOCKS, N], BF16, name="ctx2")
         wc2 = held.tile([P, CTX_BLOCKS, GATES * P], BF16, name="wc2")
-        bias_i_reset = held.tile([P, 1], F32, name="bias_i_reset")
-        bias_h_reset = held.tile([P, 1], F32, name="bias_h_reset")
-        bias_i_others = held.tile([P, GATES - 1], F32, name="bias_i_others")
-        bias_h_others = held.tile([P, GATES - 1], F32, name="bias_h_others")
-        b_i_cols = b_i.rearrange("(g m) o -> m (g o)", m=P)
-        b_h_cols = b_h.rearrange("(g m) o -> m (g o)", m=P)
+        bias_rows = held.tile([P, P], F32, name="bias_rows", align_bytes=64)
+        bias_cols = held.tile([P, P], F32, name="bias_cols", align_bytes=64)
+        nc.gpsimd.memset(bias_rows[:], 0.0)
 
-        with nc.allow_non_contiguous_dma(reason="128 biases, one to a partition"):
-            nc.sync.dma_start(bias_i_reset[:], b_i_cols[:, R : R + 1])
-            nc.sync.dma_start(bias_h_reset[:], b_h_cols[:, R : R + 1])
         nc.sync.dma_start(offsets[:], offs)
         nc.sync.dma_start(table[:], emb)
         nc.scalar.dma_start(we[:], w_e)
@@ -54,10 +50,12 @@ def tile_unsupervisedsedst_kernel(tc, emb, w_e, ctx, w_ctx, h, w_h, b_i, b_h, of
         nc.scalar.dma_start(hid[:], h)
         nc.scalar.dma_start(wh[:, reset], w_h[:, reset])
         nc.sync.dma_start(ctx2[:], ctx.rearrange("(b p) j -> p b j", p=P))
+        for row, bias in ((I, b_i), (H, b_h)):
+            nc.sync.dma_start(
+                bias_rows[row:P:BLOCK, 0 : GATES * BLOCK].rearrange("k (g j) -> k g j", j=BLOCK),
+                bias.rearrange("(g k j) o -> k g (j o)", g=GATES, j=BLOCK),
+            )
         nc.scalar.dma_start(wc2[:, :, reset], w_ctx2[:, :, reset])
-        with nc.allow_non_contiguous_dma(reason="256 biases, one to a partition and gate"):
-            nc.sync.dma_start(bias_h_others[:], b_h_cols[:, R + 1 : GATES])
-            nc.sync.dma_start(bias_i_others[:], b_i_cols[:, R + 1 : GATES])
         nc.sync.dma_start(wh[:, others], w_h[:, others])
         nc.sync.dma_start(wc2[:, :, others], w_ctx2[:, :, others])
 
@@ -65,10 +63,13 @@ def tile_unsupervisedsedst_kernel(tc, emb, w_e, ctx, w_ctx, h, w_h, b_i, b_h, of
         nc.vector.memset(early[:], 0.0)
         nc.scalar.activation(early[:], early[:], SIGMOID)
 
-        bias_sum_reset = held.tile([P, 1], F32, name="bias_sum_reset")
-        nc.vector.tensor_tensor(bias_sum_reset[:], bias_i_reset[:], bias_h_reset[:], ADD)
-        bias_sum_others = held.tile([P, GATES - 1], F32, name="bias_sum_others")
-        nc.vector.tensor_tensor(bias_sum_others[:], bias_i_others[:], bias_h_others[:], ADD)
+        nc.vector.transpose(bias_cols[:], bias_rows[:])
+        bias_i = [bias_cols[:, g * BLOCK + I : g * BLOCK + I + 1] for g in range(GATES)]
+        bias_h = [bias_cols[:, g * BLOCK + H : g * BLOCK + H + 1] for g in range(GATES)]
+        bias_sum_r = held.tile([P, 1], F32, name="bias_sum_r")
+        nc.vector.tensor_tensor(bias_sum_r[:], bias_i[R], bias_h[R], ADD)
+        bias_sum_z = held.tile([P, 1], F32, name="bias_sum_z")
+        nc.vector.tensor_tensor(bias_sum_z[:], bias_i[Z], bias_h[Z], ADD)
 
         sum_r = sums.tile([P, N], F32, name="sum_r")
         sum_z = sums.tile([P, N], F32, name="sum_z")
@@ -99,22 +100,22 @@ def tile_unsupervisedsedst_kernel(tc, emb, w_e, ctx, w_ctx, h, w_h, b_i, b_h, of
 
         r = held.tile([P, N], F32, name="r")
         for cols in pieces:
-            nc.scalar.activation(r[:, cols], sum_r[:, cols], SIGMOID, bias=bias_sum_reset[:])
+            nc.scalar.activation(r[:, cols], sum_r[:, cols], SIGMOID, bias=bias_sum_r[:])
         z = held.tile([P, N], F32, name="z")
         for cols in pieces:
-            nc.scalar.activation(z[:, cols], sum_z[:, cols], SIGMOID, bias=bias_sum_others[:, Z - 1 : Z])
+            nc.scalar.activation(z[:, cols], sum_z[:, cols], SIGMOID, bias=bias_sum_z[:])
 
         r_hc = held.tile([P, N], F32, name="r_hc")
         for cols in pieces:
             nc.vector.scalar_tensor_tensor(
-                r_hc[:, cols], sum_hc[:, cols], bias_h_others[:, C - 1 : C], r[:, cols], ADD, MULT
+                r_hc[:, cols], sum_hc[:, cols], bias_h[C], r[:, cols], ADD, MULT
             )
         pre_n = held.tile([P, N], F32, name="pre_n")
         for cols in pieces:
             nc.vector.tensor_tensor(pre_n[:, cols], r_hc[:, cols], sum_ic[:, cols], ADD)
         n = held.tile([P, N], F32, name="n")
         for cols in pieces:
-            nc.scalar.activation(n[:, cols], pre_n[:, cols], TANH, bias=bias_i_others[:, C - 1 : C])
+            nc.scalar.activation(n[:, cols], pre_n[:, cols], TANH, bias=bias_i[C])
 
         z_h = held.tile([P, N], F32, name="z_h")
         for cols in pieces:

import concourse.mybir as mybir

BF16, F32, U16 = mybir.dt.bfloat16, mybir.dt.float32, mybir.dt.uint16
ADD, SUBTRACT, MULT = mybir.AluOpType.add, mybir.AluOpType.subtract, mybir.AluOpType.mult
SIGMOID, TANH = mybir.ActivationFunctionType.Sigmoid, mybir.ActivationFunctionType.Tanh

P = 128
S = 512
N = 256
GATES = 3
R, Z, C = 0, 1, 2
BLOCK = 32
I, H = 0, 1
CTX_BLOCKS = 2
PIECES = 4

WARM = 8

FLOPS = 2 * (GATES * P) * N * ((1 + CTX_BLOCKS + 1) * P)


def tile_unsupervisedsedst_kernel(tc, emb, w_e, ctx, w_ctx, h, w_h, b_i, b_h, offs, out):
    nc = tc.nc
    with (
        tc.tile_pool(name="held", bufs=1) as held,
        tc.psum_pool(name="sums", bufs=1) as sums,
    ):
        zeros = held.tile([P, N], BF16, name="zeros")
        nc.vector.memset(zeros[:], 0.0)
        unread = sums.tile([P, N], F32, name="unread")
        for k in range(WARM):
            nc.tensor.matmul(unread[:], zeros[:, 0:P], zeros[:], start=True, stop=True)

        offsets = held.tile([P, N // 16], U16, name="offsets")
        table = held.tile([P, S], BF16, name="table")
        we = held.tile([P, GATES * P], BF16, name="we")
        hid = held.tile([P, N], BF16, name="hid")
        wh = held.tile([P, GATES * P], BF16, name="wh")
        ctx2 = held.tile([P, CTX_BLOCKS, N], BF16, name="ctx2")
        wc2 = held.tile([P, CTX_BLOCKS, GATES * P], BF16, name="wc2")
        bias_rows = held.tile([P, P], F32, name="bias_rows", align_bytes=64)
        bias_cols = held.tile([P, P], F32, name="bias_cols", align_bytes=64)
        nc.gpsimd.memset(bias_rows[:], 0.0)

        nc.sync.dma_start(offsets[:], offs)
        nc.sync.dma_start(table[:], emb)
        nc.scalar.dma_start(we[:], w_e)
        w_ctx2 = w_ctx.rearrange("(b p) m -> p b m", p=P)
        reset, others = slice(R * P, (R + 1) * P), slice((R + 1) * P, GATES * P)
        nc.scalar.dma_start(hid[:], h)
        nc.scalar.dma_start(wh[:, reset], w_h[:, reset])
        nc.sync.dma_start(ctx2[:], ctx.rearrange("(b p) j -> p b j", p=P))
        for row, bias in ((I, b_i), (H, b_h)):
            nc.sync.dma_start(
                bias_rows[row:P:BLOCK, 0 : GATES * BLOCK].rearrange("k (g j) -> k g j", j=BLOCK),
                bias.rearrange("(g k j) o -> k g (j o)", g=GATES, j=BLOCK),
            )
        nc.scalar.dma_start(wc2[:, :, reset], w_ctx2[:, :, reset])
        nc.sync.dma_start(wh[:, others], w_h[:, others])
        nc.sync.dma_start(wc2[:, :, others], w_ctx2[:, :, others])

        early = held.tile([P, 1], F32, name="early")
        nc.vector.memset(early[:], 0.0)
        nc.scalar.activation(early[:], early[:], SIGMOID)

        nc.vector.transpose(bias_cols[:], bias_rows[:])
        bias_i = [bias_cols[:, g * BLOCK + I : g * BLOCK + I + 1] for g in range(GATES)]
        bias_h = [bias_cols[:, g * BLOCK + H : g * BLOCK + H + 1] for g in range(GATES)]
        bias_sum_r = held.tile([P, 1], F32, name="bias_sum_r")
        nc.vector.tensor_tensor(bias_sum_r[:], bias_i[R], bias_h[R], ADD)
        bias_sum_z = held.tile([P, 1], F32, name="bias_sum_z")
        nc.vector.tensor_tensor(bias_sum_z[:], bias_i[Z], bias_h[Z], ADD)

        sum_r = sums.tile([P, N], F32, name="sum_r")
        sum_z = sums.tile([P, N], F32, name="sum_z")
        sum_ic = sums.tile([P, N], F32, name="sum_ic")
        sum_hc = sums.tile([P, N], F32, name="sum_hc")
        input_sums = ((R, sum_r), (C, sum_ic), (Z, sum_z))

        for g, bank in input_sums:
            nc.tensor.matmul(
                bank[:], we[:, g * P : (g + 1) * P], table[:].indirect(offsets[:]), start=True, stop=False
            )
        for g, bank in input_sums:
            if g == C:
                nc.tensor.matmul(sum_hc[:], wh[:, g * P : (g + 1) * P], hid[:], start=True, stop=True)
            else:
                nc.tensor.matmul(bank[:], wh[:, g * P : (g + 1) * P], hid[:], start=False, stop=False)
            for b in range(CTX_BLOCKS):
                nc.tensor.matmul(
                    bank[:],
                    wc2[:, b, g * P : (g + 1) * P],
                    ctx2[:, b, :],
                    start=False,
                    stop=(b == CTX_BLOCKS - 1),
                )

        halves = (slice(0, N // 2), slice(N // 2, N))
        pieces = [slice(q * N // PIECES, (q + 1) * N // PIECES) for q in range(PIECES)]

        r = held.tile([P, N], F32, name="r")
        for cols in pieces:
            nc.scalar.activation(r[:, cols], sum_r[:, cols], SIGMOID, bias=bias_sum_r[:])
        z = held.tile([P, N], F32, name="z")
        for cols in pieces:
            nc.scalar.activation(z[:, cols], sum_z[:, cols], SIGMOID, bias=bias_sum_z[:])

        r_hc = held.tile([P, N], F32, name="r_hc")
        for cols in pieces:
            nc.vector.scalar_tensor_tensor(
                r_hc[:, cols], sum_hc[:, cols], bias_h[C], r[:, cols], ADD, MULT
            )
        pre_n = held.tile([P, N], F32, name="pre_n")
        for cols in pieces:
            nc.vector.tensor_tensor(pre_n[:, cols], r_hc[:, cols], sum_ic[:, cols], ADD)
        n = held.tile([P, N], F32, name="n")
        for cols in pieces:
            nc.scalar.activation(n[:, cols], pre_n[:, cols], TANH, bias=bias_i[C])

        z_h = held.tile([P, N], F32, name="z_h")
        for cols in pieces:
            nc.vector.tensor_tensor(z_h[:, cols], z[:, cols], hid[:, cols], MULT)
        z1_n = held.tile([P, N], F32, name="z1_n")
        for cols in pieces:
            nc.vector.scalar_tensor_tensor(z1_n[:, cols], z[:, cols], 1.0, n[:, cols], SUBTRACT, MULT)
        new_h = held.tile([P, N], F32, name="new_h")
        for cols in pieces:
            nc.vector.tensor_tensor(new_h[:, cols], z_h[:, cols], z1_n[:, cols], SUBTRACT)
        for cols, queue in zip(halves, (nc.sync, nc.scalar)):
            queue.dma_start(out[:, cols], new_h[:, cols])
